import numpy as np
import ml_dtypes


def mxq(x, axis, fmt="e4m3"):
    dtype, down = {"e4m3": (ml_dtypes.float8_e4m3fn, 7), "e5m2": (ml_dtypes.float8_e5m2, 14)}[fmt]
    v = np.moveaxis(np.asarray(x, np.float32).astype(ml_dtypes.bfloat16).astype(np.float64), axis, -1)
    blocks = v.reshape(v.shape[:-1] + (-1, 32))
    amax = np.abs(blocks).max(-1, keepdims=True)
    byte = np.maximum(np.where(amax > 0, np.frexp(amax)[1] - 1 + 127, 0) - down, 1)
    scale = np.exp2(byte - 127.0)
    codes = (blocks / scale).astype(np.float32).astype(dtype).astype(np.float64)
    return np.moveaxis((codes * scale).reshape(v.shape), -1, axis)


WIDE = False


def mx_kscale(k):
    if not WIDE:
        return np.ones(k)
    levels = np.array([10, -10, 5, -5, 0])
    a = np.random.permutation(np.resize(levels, k // 512 * 4)).reshape(k // 512, 4)
    idx = np.arange(k)
    return np.exp2(a[idx // 512, idx % 128 // 32])


BF16 = ml_dtypes.bfloat16


def bf(x):
    return np.asarray(x, np.float32).astype(BF16)


def f64(x):
    return np.asarray(x).astype(np.float64)


B, D, MP, MID, L = 4096, 768, 512, 1024, 4
HALF = D // 2


def setup_inputs():
    s = mx_kscale(MP)
    t = mx_kscale(MID)
    return {
        "x": bf(np.random.standard_normal((B, D))),
        "h_prev": bf(np.maximum(np.random.standard_normal((B, MP)) * np.sqrt(2.0), 0.0) * s),
        "w_hid": bf(np.random.standard_normal((MP, MID)) * np.sqrt(2.0 / MP) / s[:, None] * t),
        "b_hid": bf(np.random.standard_normal(MID) * 0.2 * t),
        "w_out": bf(np.random.standard_normal((MID, HALF)) / np.sqrt(MID) / t[:, None]),
        "b_out": bf(np.random.standard_normal(HALF) * 0.2),
    }


def reference(x, h_prev, w_hid, b_hid, w_out, b_out):
    x = f64(x)
    first = x[:, 0::2]
    second = x[:, 1::2]
    h = np.maximum((mxq(f64(h_prev), 1, "e4m3") @ mxq(f64(w_hid), 0, "e4m3")) + f64(b_hid), 0.0)
    shift = (mxq(h, 1, "e4m3") @ mxq(f64(w_out), 0, "e4m3")) + f64(b_out)
    y_second = second + shift
    return np.stack([first, y_second], axis=2).reshape(x.shape)

@@ -1,0 +1,208 @@
+import concourse.mybir as mybir
+from concourse.masks import make_identity
+
+F32 = mybir.dt.float32
+BF16 = mybir.dt.bfloat16
+U32 = mybir.dt.uint32
+U8 = mybir.dt.uint8
+FP8X4 = mybir.dt.float8_e4m3fn_x4
+ADD = mybir.AluOpType.add
+RELU = mybir.ActivationFunctionType.Relu
+
+P = 128
+PACK = 4
+K_PASS = P * PACK
+
+TOKENS, D, MP, MID = 4096, 768, 512, 1024
+HALF = D // 2
+GROUP = 512
+TILES = GROUP // P
+N_GROUPS = TOKENS // GROUP
+MID_PASSES = MID // K_PASS
+OUT_PIECES = ((0, 256), (256, 384))
+
+FLOPS = 2 * TOKENS * (MP * MID + MID * HALF)
+
+
+def tile_additivecoupling_pa_t_kernel(tc, x, h_prev, w_hid, b_hid, w_out, b_out, out):
+    nc = tc.nc
+
+    def token_rows(dram, i):
+        return dram[i * GROUP : (i + 1) * GROUP, :].rearrange("(p t) c -> p (t c)", t=TILES)
+
+    with tc.tile_pool(name="consts", bufs=1) as consts, tc.tile_pool(
+        name="inputs", bufs=1
+    ) as inputs, tc.tile_pool(name="work", bufs=3) as work, tc.psum_pool(
+        name="psum_t", bufs=2
+    ) as psum_t, tc.psum_pool(name="psum_h", bufs=4) as psum_h, tc.psum_pool(
+        name="psum_s", bufs=2
+    ) as psum_s:
+        whid_raw = consts.tile([P, PACK, MID], BF16)
+        nc.sync.dma_start(
+            out=whid_raw[:].rearrange("q (u e) n -> q u e n", u=2),
+            in_=w_hid.rearrange("(u q e) n -> q u e n", u=2, e=2),
+        )
+        hp_tiles = []
+        x_tiles = []
+        for i in range(N_GROUPS):
+            hp_sb = inputs.tile([P, TILES * MP], BF16, name="hp%d" % i)
+            hp_tiles.append(hp_sb)
+        nc.sync.dma_start(out=hp_tiles[0][:], in_=token_rows(h_prev, 0))
+        wout_raw = consts.tile([P, MID_PASSES, PACK, HALF], BF16)
+        nc.sync.dma_start(
+            out=wout_raw[:], in_=w_out.rearrange("(g p j) n -> p g j n", g=MID_PASSES, j=PACK)
+        )
+        for i in range(N_GROUPS):
+            if i + 1 < N_GROUPS:
+                nc.sync.dma_start(out=hp_tiles[i + 1][:], in_=token_rows(h_prev, i + 1))
+            x_sb = inputs.tile([P, TILES * D], BF16, tag="x", bufs=4, name="x%d" % i)
+            nc.sync.dma_start(out=x_sb[:], in_=token_rows(x, i))
+            x_tiles.append(x_sb)
+
+        bhid_bf = consts.tile([P, MID_PASSES * PACK], BF16)
+        nc.scalar.dma_start(
+            out=bhid_bf[:].rearrange("p (g j) -> p g j", j=PACK),
+            in_=b_hid.rearrange("(g p j) -> p g j", g=MID_PASSES, j=PACK),
+        )
+        bhid = consts.tile([P, MID_PASSES * PACK], F32)
+        nc.vector.tensor_copy(out=bhid[:], in_=bhid_bf[:])
+        bout = consts.tile([P, HALF], BF16)
+        nc.scalar.dma_start(out=bout[:], in_=b_out.partition_broadcast(P))
+
+        ident = consts.tile([P, P], F32)
+        make_identity(nc, ident[:])
+
+        shift_planes = []
+        for s in range(2):
+            planes_sb = consts.tile([P, TILES, 2, HALF], F32, name="shift_planes%d" % s)
+            nc.vector.memset(planes_sb[:, :, 0, :], 0.0)
+            shift_planes.append(planes_sb)
+
+        whid_grouped = consts.tile([P, MID, PACK], BF16, align_bytes=64)
+        whid_codes = consts.tile([P, MID], U32, align_bytes=64)
+        whid_scales = consts.tile([P, MID], U8, align_bytes=64)
+        whid_sorted = whid_raw[:].rearrange("q s (g p j) -> q g j p s", g=MID_PASSES, j=PACK)
+        wout_grouped = consts.tile([P, MID_PASSES, HALF, PACK], BF16, align_bytes=64)
+        wout_codes = consts.tile([P, MID_PASSES, HALF], U32, align_bytes=64)
+        wout_scales = consts.tile([P, MID_PASSES, HALF], U8, align_bytes=64)
+        copy_of_pass = (nc.vector.tensor_copy, nc.scalar.copy)
+        for g in range(MID_PASSES):
+            cols = slice(g * K_PASS, (g + 1) * K_PASS)
+            copy_of_pass[g](
+                out=whid_grouped[:, cols, :].rearrange("q (j p) s -> q j p s", j=PACK),
+                in_=whid_sorted[:, g],
+            )
+        for g in range(MID_PASSES):
+            cols = slice(g * K_PASS, (g + 1) * K_PASS)
+            nc.vector.quantize_mx(
+                out=whid_codes[:, cols].bitcast(FP8X4),
+                scales=whid_scales[:, cols],
+                in_=whid_grouped[:, cols, :].rearrange("q c s -> q (c s)"),
+            )
+        for g in range(MID_PASSES):
+            copy_of_pass[g](
+                out=wout_grouped[:, g], in_=wout_raw[:, g].rearrange("p j n -> p n j")
+            )
+        for g in range(MID_PASSES):
+            for n0, n1 in OUT_PIECES:
+                nc.vector.quantize_mx(
+                    out=wout_codes[:, g, n0:n1].bitcast(FP8X4),
+                    scales=wout_scales[:, g, n0:n1],
+                    in_=wout_grouped[:, g, n0:n1, :].rearrange("p n j -> p (n j)"),
+                )
+
+        hp_mx = {}
+        h_mx = {}
+
+        def quantise_h_prev(i):
+            hp_words = hp_tiles[i][:].bitcast(F32)
+            hp_grouped = work.tile([P, GROUP * PACK], BF16, align_bytes=64, bufs=2)
+            grouped_words = hp_grouped[:].bitcast(F32).rearrange("q (c u) -> q c u", u=2)
+            for b in range(TILES // 2):
+                flipped = psum_t.tile([P, 2, 2 * P], F32)
+                for t2 in range(2):
+                    for u in range(2):
+                        first_word = ((2 * b + t2) * 2 + u) * P
+                        nc.tensor.transpose(
+                            flipped[:, u, t2 * P : (t2 + 1) * P],
+                            hp_words[:, first_word : first_word + P],
+                            ident[:],
+                        )
+                nc.scalar.copy(
+                    out=grouped_words[:, b * 2 * P : (b + 1) * 2 * P, :],
+                    in_=flipped[:].rearrange("q u c -> q c u"),
+                )
+            hp_codes = work.tile([P, GROUP], U32, align_bytes=64)
+            hp_scales = work.tile([P, GROUP], U8, align_bytes=64)
+            nc.vector.quantize_mx(
+                out=hp_codes[:].bitcast(FP8X4), scales=hp_scales[:], in_=hp_grouped[:]
+            )
+            hp_mx[i] = (hp_codes, hp_scales)
+
+        def hidden_layer(i):
+            hp_codes, hp_scales = hp_mx.pop(i)
+            h_codes = work.tile([P, MID_PASSES, GROUP], U32, align_bytes=64)
+            h_scales = work.tile([P, MID_PASSES, GROUP], U8, align_bytes=64)
+            for g in range(MID_PASSES):
+                h_rows = work.tile([P, PACK, GROUP], BF16)
+                for j in range(PACK):
+                    m = g * PACK + j
+                    acc = psum_h.tile([P, GROUP], F32)
+                    nc.tensor.matmul_mx(
+                        out=acc[:],
+                        lhsT=whid_codes[:, m * P : (m + 1) * P].bitcast(FP8X4),
+                        lhsT_scale=whid_scales[:, m * P : (m + 1) * P],
+                        rhs=hp_codes[:].bitcast(FP8X4),
+                        rhs_scale=hp_scales[:],
+                        start=True,
+                        stop=True,
+                    )
+                    nc.scalar.activation(
+                        out=h_rows[:, j, :], in_=acc[:], func=RELU, bias=bhid[:, m : m + 1]
+                    )
+                h_grouped = work.tile([P, GROUP, PACK], BF16, align_bytes=64)
+                copy_of_pass[g](
+                    out=h_grouped[:].rearrange("p (c i) j -> p c j i", i=4),
+                    in_=h_rows[:].rearrange("p j (c i) -> p c j i", i=4),
+                )
+                nc.vector.quantize_mx(
+                    out=h_codes[:, g, :].bitcast(FP8X4),
+                    scales=h_scales[:, g, :],
+                    in_=h_grouped[:].rearrange("p c j -> p (c j)"),
+                )
+            h_mx[i] = (h_codes, h_scales)
+
+        def output_layer(i):
+            h_codes, h_scales = h_mx.pop(i)
+            planes_sb = shift_planes[i % 2]
+            for t in range(TILES):
+                tokens = slice(t * P, (t + 1) * P)
+                acc = psum_s.tile([P, HALF], F32)
+                for n0, n1 in OUT_PIECES:
+                    for g in range(MID_PASSES):
+                        nc.tensor.matmul_mx(
+                            out=acc[:, n0:n1],
+                            lhsT=h_codes[:, g, tokens].bitcast(FP8X4),
+                            lhsT_scale=h_scales[:, g, tokens],
+                            rhs=wout_codes[:, g, n0:n1].bitcast(FP8X4),
+                            rhs_scale=wout_scales[:, g, n0:n1],
+                            start=(g == 0),
+                            stop=(g == MID_PASSES - 1),
+                        )
+                nc.vector.tensor_tensor(out=planes_sb[:, t, 1, :], in0=acc[:], in1=bout[:], op=ADD)
+            y_sb = work.tile([P, TILES * D], F32)
+            nc.vector.tensor_tensor(
+                out=y_sb[:].rearrange("p (t c e) -> p t c e", t=TILES, e=2),
+                in0=x_tiles[i][:].rearrange("p (t c e) -> p t c e", t=TILES, e=2),
+                in1=planes_sb[:].rearrange("p t e c -> p t c e"),
+                op=ADD,
+            )
+            nc.sync.dma_start(out=token_rows(out, i), in_=y_sb[:])
+
+        for step in range(N_GROUPS + 2):
+            if step < N_GROUPS:
+                quantise_h_prev(step)
+            if 1 <= step <= N_GROUPS:
+                hidden_layer(step - 1)
+            if step >= 2:
+                output_layer(step - 2)

@@ -21,6 +21,8 @@ N_GROUPS = TOKENS // GROUP
 MID_PASSES = MID // K_PASS
 OUT_PIECES = ((0, 256), (256, 384))
 
+LAG = 2
+
 FLOPS = 2 * TOKENS * (MP * MID + MID * HALF)
 
 
@@ -30,42 +32,44 @@ def tile_additivecoupling_pa_t_kernel(tc, x, h_prev, w_hid, b_hid, w_out, b_out,
     def token_rows(dram, i):
         return dram[i * GROUP : (i + 1) * GROUP, :].rearrange("(p t) c -> p (t c)", t=TILES)
 
-    with tc.tile_pool(name="consts", bufs=1) as consts, tc.tile_pool(
+    with tc.manual_schedule(), tc.tile_pool(name="consts", bufs=1) as consts, tc.tile_pool(
         name="inputs", bufs=1
     ) as inputs, tc.tile_pool(name="work", bufs=3) as work, tc.psum_pool(
         name="psum_t", bufs=2
     ) as psum_t, tc.psum_pool(name="psum_h", bufs=4) as psum_h, tc.psum_pool(
         name="psum_s", bufs=2
     ) as psum_s:
-        whid_raw = consts.tile([P, PACK, MID], BF16)
-        nc.sync.dma_start(
-            out=whid_raw[:].rearrange("q (u e) n -> q u e n", u=2),
-            in_=w_hid.rearrange("(u q e) n -> q u e n", u=2, e=2),
-        )
         hp_tiles = []
         x_tiles = []
         for i in range(N_GROUPS):
             hp_sb = inputs.tile([P, TILES * MP], BF16, name="hp%d" % i)
             hp_tiles.append(hp_sb)
+            x_sb = inputs.tile([P, TILES * D], BF16, name="x%d" % i)
+            x_tiles.append(x_sb)
         nc.sync.dma_start(out=hp_tiles[0][:], in_=token_rows(h_prev, 0))
+        whid_raw = consts.tile([P, PACK, MID], BF16)
+        for g in range(MID_PASSES):
+            cols = slice(g * K_PASS, (g + 1) * K_PASS)
+            for u in range(2):
+                nc.sync.dma_start(
+                    out=whid_raw[:, 2 * u : 2 * u + 2, cols],
+                    in_=w_hid[u * 2 * P : (u + 1) * 2 * P, cols].rearrange("(q e) n -> q e n", e=2),
+                )
+        nc.sync.dma_start(out=hp_tiles[1][:], in_=token_rows(h_prev, 1))
         wout_raw = consts.tile([P, MID_PASSES, PACK, HALF], BF16)
         nc.sync.dma_start(
             out=wout_raw[:], in_=w_out.rearrange("(g p j) n -> p g j n", g=MID_PASSES, j=PACK)
         )
         for i in range(N_GROUPS):
-            if i + 1 < N_GROUPS:
-                nc.sync.dma_start(out=hp_tiles[i + 1][:], in_=token_rows(h_prev, i + 1))
-            x_sb = inputs.tile([P, TILES * D], BF16, tag="x", bufs=4, name="x%d" % i)
-            nc.sync.dma_start(out=x_sb[:], in_=token_rows(x, i))
-            x_tiles.append(x_sb)
+            if i + 2 < N_GROUPS:
+                nc.sync.dma_start(out=hp_tiles[i + 2][:], in_=token_rows(h_prev, i + 2))
+            nc.sync.dma_start(out=x_tiles[i][:], in_=token_rows(x, i))
 
         bhid_bf = consts.tile([P, MID_PASSES * PACK], BF16)
         nc.scalar.dma_start(
             out=bhid_bf[:].rearrange("p (g j) -> p g j", j=PACK),
             in_=b_hid.rearrange("(g p j) -> p g j", g=MID_PASSES, j=PACK),
         )
-        bhid = consts.tile([P, MID_PASSES * PACK], F32)
-        nc.vector.tensor_copy(out=bhid[:], in_=bhid_bf[:])
         bout = consts.tile([P, HALF], BF16)
         nc.scalar.dma_start(out=bout[:], in_=b_out.partition_broadcast(P))
 
@@ -77,111 +81,139 @@ def tile_additivecoupling_pa_t_kernel(tc, x, h_prev, w_hid, b_hid, w_out, b_out,
             planes_sb = consts.tile([P, TILES, 2, HALF], F32, name="shift_planes%d" % s)
             nc.vector.memset(planes_sb[:, :, 0, :], 0.0)
             shift_planes.append(planes_sb)
+        bhid = consts.tile([P, MID_PASSES * PACK], F32)
+        nc.vector.tensor_copy(out=bhid[:], in_=bhid_bf[:])
 
         whid_grouped = consts.tile([P, MID, PACK], BF16, align_bytes=64)
         whid_codes = consts.tile([P, MID], U32, align_bytes=64)
         whid_scales = consts.tile([P, MID], U8, align_bytes=64)
-        whid_sorted = whid_raw[:].rearrange("q s (g p j) -> q g j p s", g=MID_PASSES, j=PACK)
         wout_grouped = consts.tile([P, MID_PASSES, HALF, PACK], BF16, align_bytes=64)
         wout_codes = consts.tile([P, MID_PASSES, HALF], U32, align_bytes=64)
         wout_scales = consts.tile([P, MID_PASSES, HALF], U8, align_bytes=64)
-        copy_of_pass = (nc.vector.tensor_copy, nc.scalar.copy)
-        for g in range(MID_PASSES):
+
+        def regroup_w_hid(g, copy):
             cols = slice(g * K_PASS, (g + 1) * K_PASS)
-            copy_of_pass[g](
+            copy(
                 out=whid_grouped[:, cols, :].rearrange("q (j p) s -> q j p s", j=PACK),
-                in_=whid_sorted[:, g],
+                in_=whid_raw[:, :, cols].rearrange("q s (p j) -> q j p s", j=PACK),
             )
-        for g in range(MID_PASSES):
+
+        def quantise_w_hid(g):
             cols = slice(g * K_PASS, (g + 1) * K_PASS)
             nc.vector.quantize_mx(
                 out=whid_codes[:, cols].bitcast(FP8X4),
                 scales=whid_scales[:, cols],
                 in_=whid_grouped[:, cols, :].rearrange("q c s -> q (c s)"),
             )
-        for g in range(MID_PASSES):
-            copy_of_pass[g](
-                out=wout_grouped[:, g], in_=wout_raw[:, g].rearrange("p j n -> p n j")
-            )
-        for g in range(MID_PASSES):
-            for n0, n1 in OUT_PIECES:
-                nc.vector.quantize_mx(
-                    out=wout_codes[:, g, n0:n1].bitcast(FP8X4),
-                    scales=wout_scales[:, g, n0:n1],
-                    in_=wout_grouped[:, g, n0:n1, :].rearrange("p n j -> p (n j)"),
+
+        def regroup_w_out():
+            for g in range(MID_PASSES):
+                nc.scalar.copy(
+                    out=wout_grouped[:, g], in_=wout_raw[:, g].rearrange("p j n -> p n j")
                 )
 
-        hp_mx = {}
-        h_mx = {}
+        def quantise_w_out():
+            for g in range(MID_PASSES):
+                for n0, n1 in OUT_PIECES:
+                    nc.vector.quantize_mx(
+                        out=wout_codes[:, g, n0:n1].bitcast(FP8X4),
+                        scales=wout_scales[:, g, n0:n1],
+                        in_=wout_grouped[:, g, n0:n1, :].rearrange("p n j -> p (n j)"),
+                    )
 
-        def quantise_h_prev(i):
+        flipped = {}
+        hp_grouped = {}
+        hp_mx = {}
+        h_acc = {}
+        h_rows = {}
+        h_grouped = {}
+        h_mx = {}
+        shift_acc = {}
+
+        def transpose_h_prev(i):
             hp_words = hp_tiles[i][:].bitcast(F32)
-            hp_grouped = work.tile([P, GROUP * PACK], BF16, align_bytes=64, bufs=2)
-            grouped_words = hp_grouped[:].bitcast(F32).rearrange("q (c u) -> q c u", u=2)
             for b in range(TILES // 2):
-                flipped = psum_t.tile([P, 2, 2 * P], F32)
+                flipped[i, b] = psum_t.tile([P, 2, 2 * P], F32, name="flipped")
                 for t2 in range(2):
                     for u in range(2):
                         first_word = ((2 * b + t2) * 2 + u) * P
                         nc.tensor.transpose(
-                            flipped[:, u, t2 * P : (t2 + 1) * P],
+                            flipped[i, b][:, u, t2 * P : (t2 + 1) * P],
                             hp_words[:, first_word : first_word + P],
                             ident[:],
                         )
+
+        def copy_h_prev(i):
+            hp_grouped[i] = work.tile(
+                [P, GROUP * PACK], BF16, align_bytes=64, bufs=2, name="hp_grouped"
+            )
+            grouped_words = hp_grouped[i][:].bitcast(F32).rearrange("q (c u) -> q c u", u=2)
+            for b in range(TILES // 2):
                 nc.scalar.copy(
                     out=grouped_words[:, b * 2 * P : (b + 1) * 2 * P, :],
-                    in_=flipped[:].rearrange("q u c -> q c u"),
+                    in_=flipped[i, b][:].rearrange("q u c -> q c u"),
                 )
+
+        def quantise_h_prev(i):
             hp_codes = work.tile([P, GROUP], U32, align_bytes=64)
             hp_scales = work.tile([P, GROUP], U8, align_bytes=64)
             nc.vector.quantize_mx(
-                out=hp_codes[:].bitcast(FP8X4), scales=hp_scales[:], in_=hp_grouped[:]
+                out=hp_codes[:].bitcast(FP8X4), scales=hp_scales[:], in_=hp_grouped[i][:]
             )
             hp_mx[i] = (hp_codes, hp_scales)
 
-        def hidden_layer(i):
-            hp_codes, hp_scales = hp_mx.pop(i)
-            h_codes = work.tile([P, MID_PASSES, GROUP], U32, align_bytes=64)
-            h_scales = work.tile([P, MID_PASSES, GROUP], U8, align_bytes=64)
-            for g in range(MID_PASSES):
-                h_rows = work.tile([P, PACK, GROUP], BF16)
-                for j in range(PACK):
-                    m = g * PACK + j
-                    acc = psum_h.tile([P, GROUP], F32)
-                    nc.tensor.matmul_mx(
-                        out=acc[:],
-                        lhsT=whid_codes[:, m * P : (m + 1) * P].bitcast(FP8X4),
-                        lhsT_scale=whid_scales[:, m * P : (m + 1) * P],
-                        rhs=hp_codes[:].bitcast(FP8X4),
-                        rhs_scale=hp_scales[:],
-                        start=True,
-                        stop=True,
-                    )
-                    nc.scalar.activation(
-                        out=h_rows[:, j, :], in_=acc[:], func=RELU, bias=bhid[:, m : m + 1]
-                    )
-                h_grouped = work.tile([P, GROUP, PACK], BF16, align_bytes=64)
-                copy_of_pass[g](
-                    out=h_grouped[:].rearrange("p (c i) j -> p c j i", i=4),
-                    in_=h_rows[:].rearrange("p j (c i) -> p c j i", i=4),
+        def hidden_matmuls(i, g):
+            hp_codes, hp_scales = hp_mx[i]
+            for j in range(PACK):
+                m = g * PACK + j
+                h_acc[i, g, j] = psum_h.tile([P, GROUP], F32, name="h_acc")
+                nc.tensor.matmul_mx(
+                    out=h_acc[i, g, j][:],
+                    lhsT=whid_codes[:, m * P : (m + 1) * P].bitcast(FP8X4),
+                    lhsT_scale=whid_scales[:, m * P : (m + 1) * P],
+                    rhs=hp_codes[:].bitcast(FP8X4),
+                    rhs_scale=hp_scales[:],
+                    start=True,
+                    stop=True,
                 )
-                nc.vector.quantize_mx(
-                    out=h_codes[:, g, :].bitcast(FP8X4),
-                    scales=h_scales[:, g, :],
-                    in_=h_grouped[:].rearrange("p c j -> p (c j)"),
-                )
-            h_mx[i] = (h_codes, h_scales)
 
-        def output_layer(i):
-            h_codes, h_scales = h_mx.pop(i)
-            planes_sb = shift_planes[i % 2]
-            for t in range(TILES):
+        def hidden_relu(i, g):
+            h_rows[i, g] = work.tile([P, PACK, GROUP], BF16, name="h_rows")
+            for j in range(PACK):
+                m = g * PACK + j
+                nc.scalar.activation(
+                    out=h_rows[i, g][:, j, :], in_=h_acc[i, g, j][:], func=RELU, bias=bhid[:, m : m + 1]
+                )
+
+        def regroup_h(i, g):
+            copy = nc.scalar.copy if (g == 1 and i >= LAG) else nc.vector.tensor_copy
+            h_grouped[i, g] = work.tile([P, GROUP, PACK], BF16, align_bytes=64, name="h_grouped")
+            copy(
+                out=h_grouped[i, g][:].rearrange("p (c i) j -> p c j i", i=4),
+                in_=h_rows[i, g][:].rearrange("p j (c i) -> p c j i", i=4),
+            )
+
+        def quantise_h(i, g):
+            if g == 0:
+                h_codes = work.tile([P, MID_PASSES, GROUP], U32, align_bytes=64)
+                h_scales = work.tile([P, MID_PASSES, GROUP], U8, align_bytes=64)
+                h_mx[i] = (h_codes, h_scales)
+            h_codes, h_scales = h_mx[i]
+            nc.vector.quantize_mx(
+                out=h_codes[:, g, :].bitcast(FP8X4),
+                scales=h_scales[:, g, :],
+                in_=h_grouped[i, g][:].rearrange("p c j -> p (c j)"),
+            )
+
+        def shift_matmuls(i, pair):
+            h_codes, h_scales = h_mx[i]
+            for t in (2 * pair, 2 * pair + 1):
                 tokens = slice(t * P, (t + 1) * P)
-                acc = psum_s.tile([P, HALF], F32)
+                shift_acc[i, t] = psum_s.tile([P, HALF], F32, name="shift_acc")
                 for n0, n1 in OUT_PIECES:
                     for g in range(MID_PASSES):
                         nc.tensor.matmul_mx(
-                            out=acc[:, n0:n1],
+                            out=shift_acc[i, t][:, n0:n1],
                             lhsT=h_codes[:, g, tokens].bitcast(FP8X4),
                             lhsT_scale=h_scales[:, g, tokens],
                             rhs=wout_codes[:, g, n0:n1].bitcast(FP8X4),
@@ -189,20 +221,57 @@ def tile_additivecoupling_pa_t_kernel(tc, x, h_prev, w_hid, b_hid, w_out, b_out,
                             start=(g == 0),
                             stop=(g == MID_PASSES - 1),
                         )
-                nc.vector.tensor_tensor(out=planes_sb[:, t, 1, :], in0=acc[:], in1=bout[:], op=ADD)
-            y_sb = work.tile([P, TILES * D], F32)
+
+        def add_b_out(i, pair):
+            for t in (2 * pair, 2 * pair + 1):
+                nc.vector.tensor_tensor(
+                    out=shift_planes[i % 2][:, t, 1, :], in0=shift_acc[i, t][:], in1=bout[:], op=ADD
+                )
+
+        def add_to_x(i, pair):
+            tiles = slice(2 * pair, 2 * pair + 2)
+            y_sb = work.tile([P, 2, HALF, 2], F32)
             nc.vector.tensor_tensor(
-                out=y_sb[:].rearrange("p (t c e) -> p t c e", t=TILES, e=2),
-                in0=x_tiles[i][:].rearrange("p (t c e) -> p t c e", t=TILES, e=2),
-                in1=planes_sb[:].rearrange("p t e c -> p t c e"),
+                out=y_sb[:],
+                in0=x_tiles[i][:].rearrange("p (t c e) -> p t c e", t=TILES, e=2)[:, tiles],
+                in1=shift_planes[i % 2][:, tiles].rearrange("p t e c -> p t c e"),
                 op=ADD,
             )
-            nc.sync.dma_start(out=token_rows(out, i), in_=y_sb[:])
+            nc.sync.dma_start(
+                out=token_rows(out, i).rearrange("p (t c) -> p t c", t=TILES)[:, tiles],
+                in_=y_sb[:].rearrange("p t c e -> p t (c e)"),
+            )
 
-        for step in range(N_GROUPS + 2):
-            if step < N_GROUPS:
-                quantise_h_prev(step)
-            if 1 <= step <= N_GROUPS:
-                hidden_layer(step - 1)
-            if step >= 2:
-                output_layer(step - 2)
+        def run(step, i, *args):
+            if 0 <= i < N_GROUPS:
+                step(i, *args)
+
+        transpose_h_prev(0)
+        copy_h_prev(0)
+        regroup_w_hid(0, nc.vector.tensor_copy)
+        regroup_w_hid(1, nc.scalar.copy)
+        quantise_w_hid(0)
+        quantise_h_prev(0)
+        hidden_matmuls(0, 0)
+        quantise_w_hid(1)
+        for i in range(N_GROUPS + LAG):
+            run(quantise_h, i - 1, 1)
+            run(transpose_h_prev, i + 1)
+            run(shift_matmuls, i - 1, 0)
+            run(hidden_relu, i, 0)
+            run(add_to_x, i - 2, 1)
+            run(add_b_out, i - 1, 0)
+            run(hidden_matmuls, i, 1)
+            run(copy_h_prev, i + 1)
+            run(regroup_h, i, 0)
+            run(quantise_h_prev, i + 1)
+            run(quantise_h, i, 0)
+            run(shift_matmuls, i - 1, 1)
+            run(hidden_relu, i, 1)
+            run(hidden_matmuls, i + 1, 0)
+            run(add_b_out, i - 1, 1)
+            run(add_to_x, i - 1, 0)
+            run(regroup_h, i, 1)
+            if i == 0:
+                regroup_w_out()
+                quantise_w_out()

@@ -91,28 +91,23 @@ def tile_additivecoupling_pa_t_kernel(tc, x, h_prev, w_hid, b_hid, w_out, b_out,
         wout_codes = consts.tile([P, MID_PASSES, HALF], U32, align_bytes=64)
         wout_scales = consts.tile([P, MID_PASSES, HALF], U8, align_bytes=64)
 
-        def regroup_w_hid(g, copy):
+        def quantise_w_hid(g):
             cols = slice(g * K_PASS, (g + 1) * K_PASS)
-            copy(
+            nc.vector.tensor_copy(
                 out=whid_grouped[:, cols, :].rearrange("q (j p) s -> q j p s", j=PACK),
                 in_=whid_raw[:, :, cols].rearrange("q s (p j) -> q j p s", j=PACK),
             )
-
-        def quantise_w_hid(g):
-            cols = slice(g * K_PASS, (g + 1) * K_PASS)
             nc.vector.quantize_mx(
                 out=whid_codes[:, cols].bitcast(FP8X4),
                 scales=whid_scales[:, cols],
                 in_=whid_grouped[:, cols, :].rearrange("q c s -> q (c s)"),
             )
 
-        def regroup_w_out():
+        def quantise_w_out():
             for g in range(MID_PASSES):
-                nc.scalar.copy(
+                nc.vector.tensor_copy(
                     out=wout_grouped[:, g], in_=wout_raw[:, g].rearrange("p j n -> p n j")
                 )
-
-        def quantise_w_out():
             for g in range(MID_PASSES):
                 for n0, n1 in OUT_PIECES:
                     nc.vector.quantize_mx(
@@ -186,7 +181,7 @@ def tile_additivecoupling_pa_t_kernel(tc, x, h_prev, w_hid, b_hid, w_out, b_out,
                 )
 
         def regroup_h(i, g):
-            copy = nc.scalar.copy if (g == 1 and i >= LAG) else nc.vector.tensor_copy
+            copy = nc.scalar.copy if (g == 1 and i > 0) else nc.vector.tensor_copy
             h_grouped[i, g] = work.tile([P, GROUP, PACK], BF16, align_bytes=64, name="h_grouped")
             copy(
                 out=h_grouped[i, g][:].rearrange("p (c i) j -> p c j i", i=4),
@@ -248,12 +243,11 @@ def tile_additivecoupling_pa_t_kernel(tc, x, h_prev, w_hid, b_hid, w_out, b_out,
 
         transpose_h_prev(0)
         copy_h_prev(0)
-        regroup_w_hid(0, nc.vector.tensor_copy)
-        regroup_w_hid(1, nc.scalar.copy)
         quantise_w_hid(0)
         quantise_h_prev(0)
         hidden_matmuls(0, 0)
         quantise_w_hid(1)
+        quantise_w_out()
         for i in range(N_GROUPS + LAG):
             run(quantise_h, i - 1, 1)
             run(transpose_h_prev, i + 1)
@@ -272,6 +266,3 @@ def tile_additivecoupling_pa_t_kernel(tc, x, h_prev, w_hid, b_hid, w_out, b_out,
             run(add_b_out, i - 1, 1)
             run(add_to_x, i - 1, 0)
             run(regroup_h, i, 1)
-            if i == 0:
-                regroup_w_out()
-                quantise_w_out()

@@ -60,18 +60,19 @@ def tile_additivecoupling_pa_t_kernel(tc, x, h_prev, w_hid, b_hid, w_out, b_out,
         nc.sync.dma_start(
             out=wout_raw[:], in_=w_out.rearrange("(g p j) n -> p g j n", g=MID_PASSES, j=PACK)
         )
+        bout = consts.tile([P, HALF], BF16)
         for i in range(N_GROUPS):
             if i + 2 < N_GROUPS:
                 nc.sync.dma_start(out=hp_tiles[i + 2][:], in_=token_rows(h_prev, i + 2))
             nc.sync.dma_start(out=x_tiles[i][:], in_=token_rows(x, i))
+            if i == 0:
+                nc.sync.dma_start(out=bout[:], in_=b_out.partition_broadcast(P))
 
         bhid_bf = consts.tile([P, MID_PASSES * PACK], BF16)
         nc.scalar.dma_start(
             out=bhid_bf[:].rearrange("p (g j) -> p g j", j=PACK),
             in_=b_hid.rearrange("(g p j) -> p g j", g=MID_PASSES, j=PACK),
         )
-        bout = consts.tile([P, HALF], BF16)
-        nc.scalar.dma_start(out=bout[:], in_=b_out.partition_broadcast(P))
 
         ident = consts.tile([P, P], F32)
         make_identity(nc, ident[:])

@@ -32,7 +32,7 @@ def tile_additivecoupling_pa_t_kernel(tc, x, h_prev, w_hid, b_hid, w_out, b_out,
     def token_rows(dram, i):
         return dram[i * GROUP : (i + 1) * GROUP, :].rearrange("(p t) c -> p (t c)", t=TILES)
 
-    with tc.manual_schedule(), tc.tile_pool(name="consts", bufs=1) as consts, tc.tile_pool(
+    with tc.tile_pool(name="consts", bufs=1) as consts, tc.tile_pool(
         name="inputs", bufs=1
     ) as inputs, tc.tile_pool(name="work", bufs=3) as work, tc.psum_pool(
         name="psum_t", bufs=2

import concourse.mybir as mybir
from concourse.masks import make_identity

F32 = mybir.dt.float32
BF16 = mybir.dt.bfloat16
U32 = mybir.dt.uint32
U8 = mybir.dt.uint8
FP8X4 = mybir.dt.float8_e4m3fn_x4
ADD = mybir.AluOpType.add
RELU = mybir.ActivationFunctionType.Relu

P = 128
PACK = 4
K_PASS = P * PACK

TOKENS, D, MP, MID = 4096, 768, 512, 1024
HALF = D // 2
GROUP = 512
TILES = GROUP // P
N_GROUPS = TOKENS // GROUP
MID_PASSES = MID // K_PASS
OUT_PIECES = ((0, 256), (256, 384))

LAG = 2

FLOPS = 2 * TOKENS * (MP * MID + MID * HALF)


def tile_additivecoupling_pa_t_kernel(tc, x, h_prev, w_hid, b_hid, w_out, b_out, out):
    nc = tc.nc

    def token_rows(dram, i):
        return dram[i * GROUP : (i + 1) * GROUP, :].rearrange("(p t) c -> p (t c)", t=TILES)

    with tc.tile_pool(name="consts", bufs=1) as consts, tc.tile_pool(
        name="inputs", bufs=1
    ) as inputs, tc.tile_pool(name="work", bufs=3) as work, tc.psum_pool(
        name="psum_t", bufs=2
    ) as psum_t, tc.psum_pool(name="psum_h", bufs=4) as psum_h, tc.psum_pool(
        name="psum_s", bufs=2
    ) as psum_s:
        hp_tiles = []
        x_tiles = []
        for i in range(N_GROUPS):
            hp_sb = inputs.tile([P, TILES * MP], BF16, name="hp%d" % i)
            hp_tiles.append(hp_sb)
            x_sb = inputs.tile([P, TILES * D], BF16, name="x%d" % i)
            x_tiles.append(x_sb)
        nc.sync.dma_start(out=hp_tiles[0][:], in_=token_rows(h_prev, 0))
        whid_raw = consts.tile([P, PACK, MID], BF16)
        for g in range(MID_PASSES):
            cols = slice(g * K_PASS, (g + 1) * K_PASS)
            for u in range(2):
                nc.sync.dma_start(
                    out=whid_raw[:, 2 * u : 2 * u + 2, cols],
                    in_=w_hid[u * 2 * P : (u + 1) * 2 * P, cols].rearrange("(q e) n -> q e n", e=2),
                )
        nc.sync.dma_start(out=hp_tiles[1][:], in_=token_rows(h_prev, 1))
        wout_raw = consts.tile([P, MID_PASSES, PACK, HALF], BF16)
        nc.sync.dma_start(
            out=wout_raw[:], in_=w_out.rearrange("(g p j) n -> p g j n", g=MID_PASSES, j=PACK)
        )
        bout = consts.tile([P, HALF], BF16)
        for i in range(N_GROUPS):
            if i + 2 < N_GROUPS:
                nc.sync.dma_start(out=hp_tiles[i + 2][:], in_=token_rows(h_prev, i + 2))
            nc.sync.dma_start(out=x_tiles[i][:], in_=token_rows(x, i))
            if i == 0:
                nc.sync.dma_start(out=bout[:], in_=b_out.partition_broadcast(P))

        bhid_bf = consts.tile([P, MID_PASSES * PACK], BF16)
        nc.scalar.dma_start(
            out=bhid_bf[:].rearrange("p (g j) -> p g j", j=PACK),
            in_=b_hid.rearrange("(g p j) -> p g j", g=MID_PASSES, j=PACK),
        )

        ident = consts.tile([P, P], F32)
        make_identity(nc, ident[:])

        shift_planes = []
        for s in range(2):
            planes_sb = consts.tile([P, TILES, 2, HALF], F32, name="shift_planes%d" % s)
            nc.vector.memset(planes_sb[:, :, 0, :], 0.0)
            shift_planes.append(planes_sb)
        bhid = consts.tile([P, MID_PASSES * PACK], F32)
        nc.vector.tensor_copy(out=bhid[:], in_=bhid_bf[:])

        whid_grouped = consts.tile([P, MID, PACK], BF16, align_bytes=64)
        whid_codes = consts.tile([P, MID], U32, align_bytes=64)
        whid_scales = consts.tile([P, MID], U8, align_bytes=64)
        wout_grouped = consts.tile([P, MID_PASSES, HALF, PACK], BF16, align_bytes=64)
        wout_codes = consts.tile([P, MID_PASSES, HALF], U32, align_bytes=64)
        wout_scales = consts.tile([P, MID_PASSES, HALF], U8, align_bytes=64)

        def quantise_w_hid(g):
            cols = slice(g * K_PASS, (g + 1) * K_PASS)
            nc.vector.tensor_copy(
                out=whid_grouped[:, cols, :].rearrange("q (j p) s -> q j p s", j=PACK),
                in_=whid_raw[:, :, cols].rearrange("q s (p j) -> q j p s", j=PACK),
            )
            nc.vector.quantize_mx(
                out=whid_codes[:, cols].bitcast(FP8X4),
                scales=whid_scales[:, cols],
                in_=whid_grouped[:, cols, :].rearrange("q c s -> q (c s)"),
            )

        def quantise_w_out():
            for g in range(MID_PASSES):
                nc.vector.tensor_copy(
                    out=wout_grouped[:, g], in_=wout_raw[:, g].rearrange("p j n -> p n j")
                )
            for g in range(MID_PASSES):
                for n0, n1 in OUT_PIECES:
                    nc.vector.quantize_mx(
                        out=wout_codes[:, g, n0:n1].bitcast(FP8X4),
                        scales=wout_scales[:, g, n0:n1],
                        in_=wout_grouped[:, g, n0:n1, :].rearrange("p n j -> p (n j)"),
                    )

        flipped = {}
        hp_grouped = {}
        hp_mx = {}
        h_acc = {}
        h_rows = {}
        h_grouped = {}
        h_mx = {}
        shift_acc = {}

        def transpose_h_prev(i):
            hp_words = hp_tiles[i][:].bitcast(F32)
            for b in range(TILES // 2):
                flipped[i, b] = psum_t.tile([P, 2, 2 * P], F32, name="flipped")
                for t2 in range(2):
                    for u in range(2):
                        first_word = ((2 * b + t2) * 2 + u) * P
                        nc.tensor.transpose(
                            flipped[i, b][:, u, t2 * P : (t2 + 1) * P],
                            hp_words[:, first_word : first_word + P],
                            ident[:],
                        )

        def copy_h_prev(i):
            hp_grouped[i] = work.tile(
                [P, GROUP * PACK], BF16, align_bytes=64, bufs=2, name="hp_grouped"
            )
            grouped_words = hp_grouped[i][:].bitcast(F32).rearrange("q (c u) -> q c u", u=2)
            for b in range(TILES // 2):
                nc.scalar.copy(
                    out=grouped_words[:, b * 2 * P : (b + 1) * 2 * P, :],
                    in_=flipped[i, b][:].rearrange("q u c -> q c u"),
                )

        def quantise_h_prev(i):
            hp_codes = work.tile([P, GROUP], U32, align_bytes=64)
            hp_scales = work.tile([P, GROUP], U8, align_bytes=64)
            nc.vector.quantize_mx(
                out=hp_codes[:].bitcast(FP8X4), scales=hp_scales[:], in_=hp_grouped[i][:]
            )
            hp_mx[i] = (hp_codes, hp_scales)

        def hidden_matmuls(i, g):
            hp_codes, hp_scales = hp_mx[i]
            for j in range(PACK):
                m = g * PACK + j
                h_acc[i, g, j] = psum_h.tile([P, GROUP], F32, name="h_acc")
                nc.tensor.matmul_mx(
                    out=h_acc[i, g, j][:],
                    lhsT=whid_codes[:, m * P : (m + 1) * P].bitcast(FP8X4),
                    lhsT_scale=whid_scales[:, m * P : (m + 1) * P],
                    rhs=hp_codes[:].bitcast(FP8X4),
                    rhs_scale=hp_scales[:],
                    start=True,
                    stop=True,
                )

        def hidden_relu(i, g):
            h_rows[i, g] = work.tile([P, PACK, GROUP], BF16, name="h_rows")
            for j in range(PACK):
                m = g * PACK + j
                nc.scalar.activation(
                    out=h_rows[i, g][:, j, :], in_=h_acc[i, g, j][:], func=RELU, bias=bhid[:, m : m + 1]
                )

        def regroup_h(i, g):
            copy = nc.scalar.copy if (g == 1 and i > 0) else nc.vector.tensor_copy
            h_grouped[i, g] = work.tile([P, GROUP, PACK], BF16, align_bytes=64, name="h_grouped")
            copy(
                out=h_grouped[i, g][:].rearrange("p (c i) j -> p c j i", i=4),
                in_=h_rows[i, g][:].rearrange("p j (c i) -> p c j i", i=4),
            )

        def quantise_h(i, g):
            if g == 0:
                h_codes = work.tile([P, MID_PASSES, GROUP], U32, align_bytes=64)
                h_scales = work.tile([P, MID_PASSES, GROUP], U8, align_bytes=64)
                h_mx[i] = (h_codes, h_scales)
            h_codes, h_scales = h_mx[i]
            nc.vector.quantize_mx(
                out=h_codes[:, g, :].bitcast(FP8X4),
                scales=h_scales[:, g, :],
                in_=h_grouped[i, g][:].rearrange("p c j -> p (c j)"),
            )

        def shift_matmuls(i, pair):
            h_codes, h_scales = h_mx[i]
            for t in (2 * pair, 2 * pair + 1):
                tokens = slice(t * P, (t + 1) * P)
                shift_acc[i, t] = psum_s.tile([P, HALF], F32, name="shift_acc")
                for n0, n1 in OUT_PIECES:
                    for g in range(MID_PASSES):
                        nc.tensor.matmul_mx(
                            out=shift_acc[i, t][:, n0:n1],
                            lhsT=h_codes[:, g, tokens].bitcast(FP8X4),
                            lhsT_scale=h_scales[:, g, tokens],
                            rhs=wout_codes[:, g, n0:n1].bitcast(FP8X4),
                            rhs_scale=wout_scales[:, g, n0:n1],
                            start=(g == 0),
                            stop=(g == MID_PASSES - 1),
                        )

        def add_b_out(i, pair):
            for t in (2 * pair, 2 * pair + 1):
                nc.vector.tensor_tensor(
                    out=shift_planes[i % 2][:, t, 1, :], in0=shift_acc[i, t][:], in1=bout[:], op=ADD
                )

        def add_to_x(i, pair):
            tiles = slice(2 * pair, 2 * pair + 2)
            y_sb = work.tile([P, 2, HALF, 2], F32)
            nc.vector.tensor_tensor(
                out=y_sb[:],
                in0=x_tiles[i][:].rearrange("p (t c e) -> p t c e", t=TILES, e=2)[:, tiles],
                in1=shift_planes[i % 2][:, tiles].rearrange("p t e c -> p t c e"),
                op=ADD,
            )
            nc.sync.dma_start(
                out=token_rows(out, i).rearrange("p (t c) -> p t c", t=TILES)[:, tiles],
                in_=y_sb[:].rearrange("p t c e -> p t (c e)"),
            )

        def run(step, i, *args):
            if 0 <= i < N_GROUPS:
                step(i, *args)

        transpose_h_prev(0)
        copy_h_prev(0)
        quantise_w_hid(0)
        quantise_h_prev(0)
        hidden_matmuls(0, 0)
        quantise_w_hid(1)
        quantise_w_out()
        for i in range(N_GROUPS + LAG):
            run(quantise_h, i - 1, 1)
            run(transpose_h_prev, i + 1)
            run(shift_matmuls, i - 1, 0)
            run(hidden_relu, i, 0)
            run(add_to_x, i - 2, 1)
            run(add_b_out, i - 1, 0)
            run(hidden_matmuls, i, 1)
            run(copy_h_prev, i + 1)
            run(regroup_h, i, 0)
            run(quantise_h_prev, i + 1)
            run(quantise_h, i, 0)
            run(shift_matmuls, i - 1, 1)
            run(hidden_relu, i, 1)
            run(hidden_matmuls, i + 1, 0)
            run(add_b_out, i - 1, 1)
            run(add_to_x, i - 1, 0)
            run(regroup_h, i, 1)
